import numpy as np
import ml_dtypes


def mxq(x, axis, fmt="e4m3"):
    dtype, down = {"e4m3": (ml_dtypes.float8_e4m3fn, 7), "e5m2": (ml_dtypes.float8_e5m2, 14)}[fmt]
    v = np.moveaxis(np.asarray(x, np.float32).astype(ml_dtypes.bfloat16).astype(np.float64), axis, -1)
    blocks = v.reshape(v.shape[:-1] + (-1, 32))
    amax = np.abs(blocks).max(-1, keepdims=True)
    byte = np.maximum(np.where(amax > 0, np.frexp(amax)[1] - 1 + 127, 0) - down, 1)
    scale = np.exp2(byte - 127.0)
    codes = (blocks / scale).astype(np.float32).astype(dtype).astype(np.float64)
    return np.moveaxis((codes * scale).reshape(v.shape), -1, axis)


WIDE = False


def mx_kscale(k):
    if not WIDE:
        return np.ones(k)
    levels = np.array([10, -10, 5, -5, 0])
    if k % 512:
        return np.exp2(np.random.permutation(np.resize(levels, k // 32))).repeat(32)
    a = np.empty((k // 512, 16))
    for p in range(k // 512):
        a[p, :8] = np.random.permutation(np.resize(levels, 8))
        for g in range(8):
            far = levels[np.abs(levels - a[p, g]) >= 10]
            a[p, g + 8] = far[np.random.randint(len(far))]
    return np.exp2(a.ravel()).repeat(32)


BF16 = ml_dtypes.bfloat16


def bf(x):
    return np.asarray(x, np.float32).astype(BF16)


def f64(x):
    return np.asarray(x).astype(np.float64)


B, C, H, W, O, HS, WS, K = 1, 8192, 32, 32, 8, 4, 4, 3
PAD = 0
NI, NJ = H // HS, W // WS


def setup_inputs():
    s = mx_kscale(C)
    fan_in = C * K * K
    return {"x": bf(np.random.standard_normal((B, C, H, W)) * s[None, :, None, None]),
            "weight": bf(np.random.standard_normal((HS, WS, O, C, K, K)) / np.sqrt(fan_in) / s[None, None, None, :, None, None]),
            "bias": bf(np.random.standard_normal((HS, WS, O)) * 0.5)}


def reference(x, weight, bias):
    x, weight = f64(x), f64(weight)
    xs = x.reshape(B, C, NI, HS, NJ, WS).transpose(3, 5, 0, 2, 4, 1).reshape(HS, WS, B * NI * NJ, C)
    ws = np.stack([np.roll(weight[:, :, :, :, u, v], (u, v), (0, 1)) for u in range(K) for v in range(K)], axis=2)
    ws = ws.transpose(0, 1, 4, 2, 3).reshape(HS, WS, C, K * K * O)
    z = mxq(xs, 3, "e4m3") @ mxq(ws, 2, "e4m3")
    zi = z.reshape(HS, WS, B, NI, NJ, K, K, O).transpose(2, 3, 0, 4, 1, 5, 6, 7).reshape(B, H, W, K, K, O)
    zp = np.pad(zi, ((0, 0), (0, WS - 2 + PAD), (0, HS - 2 + PAD), (0, 0), (0, 0), (0, 0)))
    out = sum(zp[:, u:u + H, v:v + W, u, v, :] for u in range(K) for v in range(K))
    out = out.transpose(0, 3, 1, 2).reshape(B, O, NI, HS, NJ, WS)
    out = out + f64(bias).transpose(2, 0, 1)[None, :, None, :, None, :]
    return out.reshape(B, O, H, W)

@@ -1,0 +1,238 @@
+from contextlib import ExitStack
+
+import concourse.mybir as mybir
+from concourse.masks import make_identity
+
+F32 = mybir.dt.float32
+BF16 = mybir.dt.bfloat16
+U32 = mybir.dt.uint32
+U8 = mybir.dt.uint8
+FP8X4 = mybir.dt.float8_e4m3fn_x4
+ADD = mybir.AluOpType.add
+
+P = 128
+C = 8192
+K_PASS = 512
+PASSES = C // K_PASS
+PIX = 1024
+PAT = 4
+BLK = 8
+CLASSES = PAT * PAT
+O = 8
+KS = 3
+TAPS = KS * KS
+CLS_COLS = TAPS * O
+W_COLS = CLASSES * CLS_COLS
+PAIRS = CLASSES // 2
+N_MOVE = 256
+
+LEAD = 2 * O
+
+FLOPS = 2 * PIX * CLS_COLS * C
+
+
+def window_of(pair):
+    return min(2 * CLS_COLS * pair // 64 * 64, W_COLS - N_MOVE)
+
+
+def tile_patternconv_k_kernel(tc, x, weight, bias, out):
+    nc = tc.nc
+    x_view = x.rearrange("b (g k t) y z -> g k (b t y z)", g=PASSES, k=P, t=4)
+    w_view = weight.rearrange("h w o (g c) u v -> g (h w o) (c u v)", g=PASSES)
+    out_view = out.rearrange("b o (i h) z -> h (b o) i z", h=PAT)
+
+    with ExitStack() as ctx:
+        const = ctx.enter_context(tc.tile_pool(name="const", bufs=1))
+        loads = ctx.enter_context(tc.tile_pool(name="loads", bufs=3))
+        stage = ctx.enter_context(tc.tile_pool(name="stage", bufs=2))
+        codes = ctx.enter_context(tc.tile_pool(name="codes", bufs=3))
+        flip_psum = ctx.enter_context(tc.psum_pool(name="flip_psum", bufs=4))
+        z_psum = ctx.enter_context(tc.psum_pool(name="z_psum", bufs=1))
+
+        ident = const.tile([P, P], F32)
+        make_identity(nc, ident[:])
+        twice = const.tile([P, 2 * PAT, 2 * PAT, O], F32)
+        ident_hwo = ident[:].rearrange("k (h w o) -> k h w o", h=PAT, w=PAT)
+        for a in range(2):
+            for b in range(2):
+                nc.vector.tensor_copy(
+                    out=twice[:, PAT * a : PAT * (a + 1), PAT * b : PAT * (b + 1), :], in_=ident_hwo
+                )
+        perm = const.tile([P, TAPS, P], F32)
+        for u in range(KS):
+            for v in range(KS):
+                nc.vector.tensor_copy(
+                    out=perm[:, KS * u + v, :].rearrange("k (p q o) -> k p q o", p=PAT, q=PAT),
+                    in_=twice[:, PAT - u : 2 * PAT - u, PAT - v : 2 * PAT - v, :],
+                )
+        block_of = const.tile([P, BLK + 1, BLK + 1], F32)
+        nc.vector.memset(block_of[:], 0.0)
+        nc.vector.tensor_tensor(
+            out=block_of[:, 0:BLK, 0:BLK],
+            in0=ident[:, 0:64].rearrange("k (i j) -> k i j", i=BLK),
+            in1=ident[:, 64:128].rearrange("k (i j) -> k i j", i=BLK),
+            op=ADD,
+        )
+        shift = const.tile([P, 4, BLK * BLK], F32)
+        for di in range(2):
+            for dj in range(2):
+                nc.vector.tensor_copy(
+                    out=shift[:, 2 * di + dj, :].rearrange("k (i j) -> k i j", i=BLK),
+                    in_=block_of[:, di : di + BLK, dj : dj + BLK],
+                )
+        patch = const.tile([P, 512], F32)
+        nc.vector.memset(patch[:], 0.0)
+        patch_abo = patch[:, LEAD : LEAD + 6 * 8 * O].rearrange("k (b a o) -> k a b o", b=6, a=8)
+        bias_rows = const.tile([64, CLASSES * O], BF16)
+        nc.scalar.dma_start(out=bias_rows[:], in_=bias.rearrange("h w o -> (h w o)").partition_broadcast(64))
+        nc.vector.tensor_copy(
+            out=patch_abo[0:64, 2 : 2 + PAT, 2 : 2 + PAT, :],
+            in_=bias_rows[:].rearrange("k (h w o) -> k h w o", h=PAT, w=PAT),
+        )
+
+        z_banks = [z_psum.tile([P, 2, N_MOVE], F32, name="z_bank%d" % b) for b in range(PAIRS // 2)]
+        held = {}
+
+        def load(g):
+            w_nat = loads.tile([P, K_PASS * TAPS], BF16)
+            nc.sync.dma_start(out=w_nat[:], in_=w_view[g])
+            x_raw = loads.tile([P, 4, PIX], BF16)
+            nc.sync.dma_start(out=x_raw[:].rearrange("k t n -> k (t n)"), in_=x_view[g])
+            held["w_nat", g] = w_nat
+            held["x_raw", g] = x_raw
+
+        def sort_taps(g):
+            w_tap = stage.tile([P, TAPS, K_PASS], BF16, align_bytes=64)
+            w_nat_ct = held["w_nat", g][:].rearrange("k (c t) -> k c t", t=TAPS)
+            w_tap_ct = w_tap[:].rearrange("k t c -> k c t")
+            nc.vector.tensor_copy(out=w_tap_ct[:, :, 0:3], in_=w_nat_ct[:, :, 0:3])
+            nc.scalar.copy(out=w_tap_ct[:, :, 3:6], in_=w_nat_ct[:, :, 3:6])
+            nc.scalar.copy(out=w_tap_ct[:, :, 6:9], in_=w_nat_ct[:, :, 6:9])
+            held["w_tap", g] = w_tap
+
+        def group_x(g):
+            x_grp = stage.tile([P, PIX, 4], BF16, align_bytes=64)
+            x_raw_sorted = held["x_raw", g][:].rearrange(
+                "k t (i p j q) -> k p i j t q", i=BLK, p=PAT, j=BLK, q=PAT
+            )
+            for p in range(PAT):
+                nc.vector.tensor_copy(
+                    out=x_grp[:, 256 * p : 256 * (p + 1), :].rearrange(
+                        "k (q i j) t -> k i j t q", q=PAT, i=BLK
+                    ),
+                    in_=x_raw_sorted[:, p],
+                )
+            held["x_grp", g] = x_grp
+
+        def flip(g):
+            w_tap_words = held["w_tap", g][:].bitcast(F32)
+            w_grp = stage.tile([P, W_COLS * 4], BF16, align_bytes=64)
+            w_grp_words = w_grp[:].bitcast(F32).rearrange(
+                "k (c t o u) -> k t c o u", c=CLASSES, t=TAPS, o=O, u=2
+            )
+            for tap0 in range(0, TAPS, 2):
+                flipped = flip_psum.tile([P, 2, 2, P], F32, tag="flipped")
+                taps_here = range(tap0, min(tap0 + 2, TAPS))
+                for tap in taps_here:
+                    for u2 in range(2):
+                        nc.tensor.transpose(
+                            flipped[:, tap - tap0, u2, :],
+                            w_tap_words[:, tap, u2 : 2 * P : 2],
+                            perm[:, tap, :],
+                        )
+                for tap in taps_here:
+                    nc.scalar.copy(
+                        out=w_grp_words[:, TAPS - 1 - tap],
+                        in_=flipped[:, tap - tap0, :, :].rearrange("k u (c o) -> k c o u", c=CLASSES),
+                    )
+            held["w_grp", g] = w_grp
+
+        def quantise_x(g):
+            x_codes = codes.tile([P, PIX], U32, align_bytes=64)
+            x_scales = codes.tile([P, PIX], U8, align_bytes=64)
+            nc.vector.quantize_mx(
+                out=x_codes[:].bitcast(FP8X4),
+                scales=x_scales[:],
+                in_=held["x_grp", g][:].rearrange("k c t -> k (c t)"),
+            )
+            held["x_mx", g] = (x_codes, x_scales)
+
+        def quantise_w(g):
+            w_grp = held["w_grp", g]
+            w_codes = codes.tile([P, W_COLS], U32, align_bytes=64)
+            w_scales = codes.tile([P, W_COLS], U8, align_bytes=64)
+            for c0, c1 in ((0, 1024), (1024, W_COLS)):
+                nc.vector.quantize_mx(
+                    out=w_codes[:, c0:c1].bitcast(FP8X4),
+                    scales=w_scales[:, c0:c1],
+                    in_=w_grp[:, 4 * c0 : 4 * c1],
+                )
+            held["w_mx", g] = (w_codes, w_scales)
+
+        def multiply(g):
+            x_codes, x_scales = held["x_mx", g]
+            w_codes, w_scales = held["w_mx", g]
+            for pair in range(PAIRS):
+                window = window_of(pair)
+                nc.tensor.matmul_mx(
+                    out=z_banks[pair // 2][:, pair % 2, :],
+                    lhsT=x_codes[:, P * pair : P * (pair + 1)].bitcast(FP8X4),
+                    lhsT_scale=x_scales[:, P * pair : P * (pair + 1)],
+                    rhs=w_codes[:, window : window + N_MOVE].bitcast(FP8X4),
+                    rhs_scale=w_scales[:, window : window + N_MOVE],
+                    start=(g == 0 and pair % 2 == 0),
+                    stop=(g == PASSES - 1 and pair % 2 == 1),
+                )
+
+        for step in range(PASSES + 3):
+            if step < PASSES:
+                load(step)
+            if 0 <= step - 1 < PASSES:
+                sort_taps(step - 1)
+                group_x(step - 1)
+            if 0 <= step - 2 < PASSES:
+                flip(step - 2)
+                quantise_x(step - 2)
+            if 0 <= step - 3 < PASSES:
+                quantise_w(step - 3)
+                multiply(step - 3)
+
+        for pair in range(PAIRS):
+            for half in range(2):
+                cls = 2 * pair + half
+                p, q = cls // PAT, cls % PAT
+                rows = slice(64 * half, 64 * (half + 1))
+                mine = CLS_COLS * cls - window_of(pair)
+                cell = patch_abo[rows, p : p + KS, q : q + KS, :]
+                nc.vector.tensor_tensor(
+                    out=cell,
+                    in0=z_banks[pair // 2][rows, pair % 2, mine : mine + CLS_COLS].rearrange(
+                        "k (a b o) -> k a b o", a=KS, b=KS
+                    ),
+                    in1=cell,
+                    op=ADD,
+                )
+
+        total = flip_psum.tile([P, PAT, BLK * BLK], F32, tag="flipped")
+        for w in range(PAT):
+            terms = [(di, dj) for dj in range(2 if w >= 2 else 1) for di in range(2)]
+            for n, (di, dj) in enumerate(terms):
+                b = w + 2 - PAT * dj
+                col = LEAD + 8 * O * b + (2 * O if di == 0 else -2 * O)
+                nc.tensor.matmul(
+                    total[:, w, :],
+                    lhsT=patch[:, col : col + P],
+                    rhs=shift[:, 2 * di + dj, :],
+                    start=(n == 0),
+                    stop=(n == len(terms) - 1),
+                )
+        result = const.tile([PAT * O, BLK * BLK * PAT], F32)
+        nc.vector.tensor_copy(
+            out=result[:].rearrange("k (n w) -> k n w", w=PAT),
+            in_=total[0 : PAT * O, :, :].rearrange("k w n -> k n w"),
+        )
+        for h in range(PAT):
+            nc.sync.dma_start(
+                out=out_view[h],
+                in_=result[O * h : O * (h + 1), :].rearrange("k (i z) -> k i z", i=BLK),
+            )

@@ -136,15 +136,15 @@ def tile_patternconv_k_kernel(tc, x, weight, bias, out):
                 for tap in taps_here:
                     for u2 in range(2):
                         nc.tensor.transpose(
-                            flipped[:, tap - tap0, u2, :],
+                            flipped[:, taps_here[-1] - tap, u2, :],
                             w_tap_words[:, tap, u2 : 2 * P : 2],
                             perm[:, tap, :],
                         )
-                for tap in taps_here:
-                    nc.scalar.copy(
-                        out=w_grp_words[:, TAPS - 1 - tap],
-                        in_=flipped[:, tap - tap0, :, :].rearrange("k u (c o) -> k c o u", c=CLASSES),
-                    )
+                first_col = TAPS - 1 - taps_here[-1]
+                nc.scalar.copy(
+                    out=w_grp_words[:, first_col : first_col + len(taps_here)],
+                    in_=flipped[:, 0 : len(taps_here)].rearrange("k t u (c o) -> k t c o u", c=CLASSES),
+                )
             held["w_grp", g] = w_grp
 
         def quantise_x(g):

@@ -9,6 +9,8 @@ U32 = mybir.dt.uint32
 U8 = mybir.dt.uint8
 FP8X4 = mybir.dt.float8_e4m3fn_x4
 ADD = mybir.AluOpType.add
+MULT = mybir.AluOpType.mult
+AXIS_X = mybir.AxisListType.X
 
 P = 128
 C = 8192
@@ -24,9 +26,8 @@ TAPS = KS * KS
 CLS_COLS = TAPS * O
 W_COLS = CLASSES * CLS_COLS
 PAIRS = CLASSES // 2
+TAP_ORDER = [KS * (KS - 1 - a) + (KS - 1 - b) for b in range(KS) for a in range(KS)]
 N_MOVE = 256
-
-LEAD = 2 * O
 
 FLOPS = 2 * PIX * CLS_COLS * C
 
@@ -37,20 +38,46 @@ def window_of(pair):
 
 def tile_patternconv_k_kernel(tc, x, weight, bias, out):
     nc = tc.nc
-    x_view = x.rearrange("b (g k t) y z -> g k (b t y z)", g=PASSES, k=P, t=4)
+    x_view = x.rearrange("b (g k t) y z -> g k t (b y z)", g=PASSES, k=P, t=4)
     w_view = weight.rearrange("h w o (g c) u v -> g (h w o) (c u v)", g=PASSES)
     out_view = out.rearrange("b o (i h) z -> h (b o) i z", h=PAT)
 
     with ExitStack() as ctx:
         const = ctx.enter_context(tc.tile_pool(name="const", bufs=1))
-        loads = ctx.enter_context(tc.tile_pool(name="loads", bufs=3))
-        stage = ctx.enter_context(tc.tile_pool(name="stage", bufs=2))
+        loads = ctx.enter_context(tc.tile_pool(name="loads", bufs=4))
+        stage = ctx.enter_context(tc.tile_pool(name="stage", bufs=3))
         codes = ctx.enter_context(tc.tile_pool(name="codes", bufs=3))
         flip_psum = ctx.enter_context(tc.psum_pool(name="flip_psum", bufs=4))
         z_psum = ctx.enter_context(tc.psum_pool(name="z_psum", bufs=1))
+        ctx.enter_context(tc.manual_schedule())
+
+        held = {}
+
+        def load(g, pieces):
+            w_nat = loads.tile([P, K_PASS * TAPS], BF16)
+            x_raw = loads.tile([P, 4, PIX], BF16)
+            w_cols = K_PASS * TAPS // pieces
+            x_cols = PIX // pieces
+            for n in range(pieces):
+                cols = slice(w_cols * n, w_cols * (n + 1))
+                nc.sync.dma_start(out=w_nat[:, cols], in_=w_view[g][:, cols])
+                cols = slice(x_cols * n, x_cols * (n + 1))
+                nc.sync.dma_start(out=x_raw[:, :, cols], in_=x_view[g][:, :, cols])
+            held["w_nat", g] = w_nat
+            held["x_raw", g] = x_raw
+
+        AHEAD = 3
+        for g in range(AHEAD):
+            load(g, 2 if g == 0 else 1)
 
         ident = const.tile([P, P], F32)
         make_identity(nc, ident[:])
+        patch = const.tile([P, 2 * PAT, 2 * PAT * O], F32)
+        nc.gpsimd.memset(patch[:], 0.0)
+        outer = const.tile([P, 2 * P - PAT * O], F32)
+        nc.gpsimd.memset(outer[:], 0.0)
+        bias_rows = const.tile([P, CLASSES * O], BF16)
+        nc.scalar.dma_start(out=bias_rows[:], in_=bias.rearrange("h w o -> (h w o)").partition_broadcast(P))
         twice = const.tile([P, 2 * PAT, 2 * PAT, O], F32)
         ident_hwo = ident[:].rearrange("k (h w o) -> k h w o", h=PAT, w=PAT)
         for a in range(2):
@@ -62,67 +89,48 @@ def tile_patternconv_k_kernel(tc, x, weight, bias, out):
         for u in range(KS):
             for v in range(KS):
                 nc.vector.tensor_copy(
-                    out=perm[:, KS * u + v, :].rearrange("k (p q o) -> k p q o", p=PAT, q=PAT),
-                    in_=twice[:, PAT - u : 2 * PAT - u, PAT - v : 2 * PAT - v, :],
+                    out=perm[:, KS * u + v, :].rearrange("k (d p e o) -> k p d (e o)", d=2, p=PAT, e=2),
+                    in_=twice[:, PAT - u : 2 * PAT - u, PAT - v : 2 * PAT - v, :].rearrange(
+                        "k p (d e) o -> k p d (e o)", d=2
+                    ),
                 )
+        is_e = const.tile([P, 2], F32)
+        ident_ije = ident[:].rearrange("k (n e) -> k e n", e=2)
+        for e in range(2):
+            nc.vector.tensor_reduce(out=is_e[:, e : e + 1], in_=ident_ije[:, e, :], op=ADD, axis=AXIS_X)
         block_of = const.tile([P, BLK + 1, BLK + 1], F32)
         nc.vector.memset(block_of[:], 0.0)
         nc.vector.tensor_tensor(
             out=block_of[:, 0:BLK, 0:BLK],
-            in0=ident[:, 0:64].rearrange("k (i j) -> k i j", i=BLK),
-            in1=ident[:, 64:128].rearrange("k (i j) -> k i j", i=BLK),
+            in0=ident_ije[:, 0, :].rearrange("k (i j) -> k i j", i=BLK),
+            in1=ident_ije[:, 1, :].rearrange("k (i j) -> k i j", i=BLK),
             op=ADD,
         )
-        shift = const.tile([P, 4, BLK * BLK], F32)
+        shift = const.tile([P, 4, P], F32)
+        nc.vector.memset(shift[:], 0.0)
         for di in range(2):
             for dj in range(2):
                 nc.vector.tensor_copy(
-                    out=shift[:, 2 * di + dj, :].rearrange("k (i j) -> k i j", i=BLK),
+                    out=shift[:, 2 * di + dj, 0 : BLK * BLK].rearrange("k (i j) -> k i j", i=BLK),
                     in_=block_of[:, di : di + BLK, dj : dj + BLK],
                 )
-        patch = const.tile([P, 512], F32)
-        nc.vector.memset(patch[:], 0.0)
-        patch_abo = patch[:, LEAD : LEAD + 6 * 8 * O].rearrange("k (b a o) -> k a b o", b=6, a=8)
-        bias_rows = const.tile([64, CLASSES * O], BF16)
-        nc.scalar.dma_start(out=bias_rows[:], in_=bias.rearrange("h w o -> (h w o)").partition_broadcast(64))
-        nc.vector.tensor_copy(
-            out=patch_abo[0:64, 2 : 2 + PAT, 2 : 2 + PAT, :],
-            in_=bias_rows[:].rearrange("k (h w o) -> k h w o", h=PAT, w=PAT),
-        )
+        z_banks = [z_psum.tile([P, 2, N_MOVE], F32, name="z_bank%d" % p) for p in range(PAT)]
 
-        z_banks = [z_psum.tile([P, 2, N_MOVE], F32, name="z_bank%d" % b) for b in range(PAIRS // 2)]
-        held = {}
+        def sort_taps(g, taps, engine_copy, pieces):
+            w_nat = held["w_nat", g][:].rearrange("p (k u e t) -> p u k e t", k=P, u=2, e=2)
+            w_tap = held["w_tap", g][:].rearrange("p t (u k e) -> p u k e t", u=2, e=2)
+            rows = P // pieces
+            for n in range(pieces):
+                ks = slice(rows * n, rows * (n + 1))
+                engine_copy(out=w_tap[:, :, ks, :, taps], in_=w_nat[:, :, ks, :, taps])
 
-        def load(g):
-            w_nat = loads.tile([P, K_PASS * TAPS], BF16)
-            nc.sync.dma_start(out=w_nat[:], in_=w_view[g])
-            x_raw = loads.tile([P, 4, PIX], BF16)
-            nc.sync.dma_start(out=x_raw[:].rearrange("k t n -> k (t n)"), in_=x_view[g])
-            held["w_nat", g] = w_nat
-            held["x_raw", g] = x_raw
-
-        def sort_taps(g):
-            w_tap = stage.tile([P, TAPS, K_PASS], BF16, align_bytes=64)
-            w_nat_ct = held["w_nat", g][:].rearrange("k (c t) -> k c t", t=TAPS)
-            w_tap_ct = w_tap[:].rearrange("k t c -> k c t")
-            nc.vector.tensor_copy(out=w_tap_ct[:, :, 0:3], in_=w_nat_ct[:, :, 0:3])
-            nc.scalar.copy(out=w_tap_ct[:, :, 3:6], in_=w_nat_ct[:, :, 3:6])
-            nc.scalar.copy(out=w_tap_ct[:, :, 6:9], in_=w_nat_ct[:, :, 6:9])
-            held["w_tap", g] = w_tap
-
-        def group_x(g):
-            x_grp = stage.tile([P, PIX, 4], BF16, align_bytes=64)
-            x_raw_sorted = held["x_raw", g][:].rearrange(
-                "k t (i p j q) -> k p i j t q", i=BLK, p=PAT, j=BLK, q=PAT
-            )
-            for p in range(PAT):
-                nc.vector.tensor_copy(
-                    out=x_grp[:, 256 * p : 256 * (p + 1), :].rearrange(
-                        "k (q i j) t -> k i j t q", q=PAT, i=BLK
-                    ),
-                    in_=x_raw_sorted[:, p],
-                )
-            held["x_grp", g] = x_grp
+        def group_x(g, p, pieces):
+            x_raw = held["x_raw", g][:].rearrange("k t (i p j d e) -> k p i j t d e", i=BLK, p=PAT, j=BLK, d=2)
+            x_grp = held["x_grp", g][:].rearrange("k (d p i j e) t -> k p i j t d e", d=2, p=PAT, i=BLK, j=BLK)
+            rows = BLK // pieces
+            for n in range(pieces):
+                i_rows = slice(rows * n, rows * (n + 1))
+                nc.vector.tensor_copy(out=x_grp[:, p, i_rows], in_=x_raw[:, p, i_rows])
 
         def flip(g):
             w_tap_words = held["w_tap", g][:].bitcast(F32)
@@ -130,19 +138,18 @@ def tile_patternconv_k_kernel(tc, x, weight, bias, out):
             w_grp_words = w_grp[:].bitcast(F32).rearrange(
                 "k (c t o u) -> k t c o u", c=CLASSES, t=TAPS, o=O, u=2
             )
-            for tap0 in range(0, TAPS, 2):
+            for n0 in range(0, TAPS, 2):
                 flipped = flip_psum.tile([P, 2, 2, P], F32, tag="flipped")
-                taps_here = range(tap0, min(tap0 + 2, TAPS))
-                for tap in taps_here:
-                    for u2 in range(2):
+                taps_here = TAP_ORDER[n0 : n0 + 2]
+                for n, tap in enumerate(taps_here):
+                    for u in range(2):
                         nc.tensor.transpose(
-                            flipped[:, taps_here[-1] - tap, u2, :],
-                            w_tap_words[:, tap, u2 : 2 * P : 2],
+                            flipped[:, n, u, :],
+                            w_tap_words[:, tap, P * u : P * (u + 1)],
                             perm[:, tap, :],
                         )
-                first_col = TAPS - 1 - taps_here[-1]
                 nc.scalar.copy(
-                    out=w_grp_words[:, first_col : first_col + len(taps_here)],
+                    out=w_grp_words[:, n0 : n0 + len(taps_here)],
                     in_=flipped[:, 0 : len(taps_here)].rearrange("k t u (c o) -> k t c o u", c=CLASSES),
                 )
             held["w_grp", g] = w_grp
@@ -157,11 +164,11 @@ def tile_patternconv_k_kernel(tc, x, weight, bias, out):
             )
             held["x_mx", g] = (x_codes, x_scales)
 
-        def quantise_w(g):
+        def quantise_w(g, cuts):
             w_grp = held["w_grp", g]
             w_codes = codes.tile([P, W_COLS], U32, align_bytes=64)
             w_scales = codes.tile([P, W_COLS], U8, align_bytes=64)
-            for c0, c1 in ((0, 1024), (1024, W_COLS)):
+            for c0, c1 in zip(cuts[:-1], cuts[1:]):
                 nc.vector.quantize_mx(
                     out=w_codes[:, c0:c1].bitcast(FP8X4),
                     scales=w_scales[:, c0:c1],
@@ -172,67 +179,89 @@ def tile_patternconv_k_kernel(tc, x, weight, bias, out):
         def multiply(g):
             x_codes, x_scales = held["x_mx", g]
             w_codes, w_scales = held["w_mx", g]
-            for pair in range(PAIRS):
-                window = window_of(pair)
-                nc.tensor.matmul_mx(
-                    out=z_banks[pair // 2][:, pair % 2, :],
-                    lhsT=x_codes[:, P * pair : P * (pair + 1)].bitcast(FP8X4),
-                    lhsT_scale=x_scales[:, P * pair : P * (pair + 1)],
-                    rhs=w_codes[:, window : window + N_MOVE].bitcast(FP8X4),
-                    rhs_scale=w_scales[:, window : window + N_MOVE],
-                    start=(g == 0 and pair % 2 == 0),
-                    stop=(g == PASSES - 1 and pair % 2 == 1),
-                )
+            for p in range(PAT):
+                for d in range(2):
+                    pair = PAT * d + p
+                    window = window_of(pair)
+                    nc.tensor.matmul_mx(
+                        out=z_banks[p][:, d, :],
+                        lhsT=x_codes[:, P * pair : P * (pair + 1)].bitcast(FP8X4),
+                        lhsT_scale=x_scales[:, P * pair : P * (pair + 1)],
+                        rhs=w_codes[:, window : window + N_MOVE].bitcast(FP8X4),
+                        rhs_scale=w_scales[:, window : window + N_MOVE],
+                        start=(g == 0 and d == 0),
+                        stop=(g == PASSES - 1 and d == 1),
+                    )
 
-        for step in range(PASSES + 3):
+        for step in range(PASSES + 2):
+            pieces = 2 if step == 0 else 1
+            if AHEAD <= step + AHEAD - 1 < PASSES:
+                load(step + AHEAD - 1, 1)
             if step < PASSES:
-                load(step)
+                held["w_tap", step] = stage.tile([P, TAPS, K_PASS], BF16, align_bytes=64, name="w_tap")
+                held["x_grp", step] = stage.tile([P, PIX, 4], BF16, align_bytes=64, name="x_grp")
+                sort_taps(step, slice(0, 3), nc.vector.tensor_copy, pieces)
+                sort_taps(step, slice(3, 6), nc.scalar.copy, pieces)
+                sort_taps(step, slice(6, 9), nc.scalar.copy, pieces)
+                group_x(step, 0, pieces)
+                group_x(step, 1, pieces)
             if 0 <= step - 1 < PASSES:
-                sort_taps(step - 1)
-                group_x(step - 1)
+                flip(step - 1)
             if 0 <= step - 2 < PASSES:
-                flip(step - 2)
-                quantise_x(step - 2)
-            if 0 <= step - 3 < PASSES:
-                quantise_w(step - 3)
-                multiply(step - 3)
+                quantise_w(step - 2, (0, 512, 1024, W_COLS) if step - 2 == PASSES - 1 else (0, 1024, W_COLS))
+                multiply(step - 2)
+            if step < PASSES:
+                group_x(step, 2, pieces)
+                group_x(step, 3, pieces)
+            if 0 <= step - 1 < PASSES:
+                quantise_x(step - 1)
 
-        for pair in range(PAIRS):
-            for half in range(2):
-                cls = 2 * pair + half
-                p, q = cls // PAT, cls % PAT
-                rows = slice(64 * half, 64 * (half + 1))
-                mine = CLS_COLS * cls - window_of(pair)
-                cell = patch_abo[rows, p : p + KS, q : q + KS, :]
-                nc.vector.tensor_tensor(
-                    out=cell,
-                    in0=z_banks[pair // 2][rows, pair % 2, mine : mine + CLS_COLS].rearrange(
-                        "k (a b o) -> k a b o", a=KS, b=KS
-                    ),
-                    in1=cell,
-                    op=ADD,
-                )
+        for p in range(PAT):
+            for e in range(2):
+                for d in range(2):
+                    pair = PAT * d + p
+                    mine = CLS_COLS * (2 * pair + e) - window_of(pair)
+                    cell = patch[:, PAT * d + e : PAT * d + e + KS, O * (p + 2) : O * (p + 2 + KS)]
+                    nc.vector.scalar_tensor_tensor(
+                        out=cell,
+                        in0=z_banks[p][:, d, mine : mine + CLS_COLS].rearrange("k (b n) -> k b n", b=KS),
+                        scalar=is_e[:, e : e + 1],
+                        in1=cell,
+                        op0=MULT,
+                        op1=ADD,
+                    )
+        nc.vector.tensor_tensor(
+            out=patch[:, PAT : PAT + 2, :], in0=patch[:, PAT : PAT + 2, :], in1=patch[:, 2:PAT, :], op=ADD
+        )
 
-        total = flip_psum.tile([P, PAT, BLK * BLK], F32, tag="flipped")
+        total = flip_psum.tile([P, PAT, PAT * O], F32, tag="flipped")
+        terms = [(di, dj) for dj in range(2) for di in range(2)]
+        for n, (di, dj) in enumerate(terms):
+            w0 = 2 * dj
+            rows = slice(PAT * O * (1 - di), PAT * O * (2 - di))
+            nc.tensor.matmul(
+                total[:, w0:PAT, :],
+                lhsT=shift[:, 2 * di + dj, :],
+                rhs=patch[:, 0:2, rows] if dj else patch[:, PAT : 2 * PAT, rows],
+                start=(n == 0),
+                stop=(n == len(terms) - 1),
+            )
+        nc.vector.tensor_tensor(
+            out=outer[:, 0:P].rearrange("k (w h o) -> k w h o", w=PAT, h=PAT),
+            in0=total[:].rearrange("k w (h o) -> k w h o", h=PAT),
+            in1=bias_rows[:].rearrange("k (h w o) -> k w h o", h=PAT, w=PAT),
+            op=ADD,
+        )
+        turned = flip_psum.tile([P, PAT, P], F32, tag="flipped")
         for w in range(PAT):
-            terms = [(di, dj) for dj in range(2 if w >= 2 else 1) for di in range(2)]
-            for n, (di, dj) in enumerate(terms):
-                b = w + 2 - PAT * dj
-                col = LEAD + 8 * O * b + (2 * O if di == 0 else -2 * O)
-                nc.tensor.matmul(
-                    total[:, w, :],
-                    lhsT=patch[:, col : col + P],
-                    rhs=shift[:, 2 * di + dj, :],
-                    start=(n == 0),
-                    stop=(n == len(terms) - 1),
-                )
-        result = const.tile([PAT * O, BLK * BLK * PAT], F32)
+            nc.tensor.transpose(turned[:, w, :], outer[:, PAT * O * w : PAT * O * w + P], ident[:])
+        result = const.tile([PAT * O, BLK * BLK, PAT], F32)
         nc.vector.tensor_copy(
-            out=result[:].rearrange("k (n w) -> k n w", w=PAT),
-            in_=total[0 : PAT * O, :, :].rearrange("k w n -> k n w"),
+            out=result[:], in_=turned[0 : PAT * O, :, 0 : BLK * BLK].rearrange("k w n -> k n w")
         )
         for h in range(PAT):
-            nc.sync.dma_start(
+            queue = nc.sync if h % 2 == 0 else nc.scalar
+            queue.dma_start(
                 out=out_view[h],
-                in_=result[O * h : O * (h + 1), :].rearrange("k (i z) -> k i z", i=BLK),
+                in_=result[O * h : O * (h + 1)].rearrange("k (i j) w -> k i (j w)", i=BLK),
             )

@@ -27,6 +27,7 @@ CLS_COLS = TAPS * O
 W_COLS = CLASSES * CLS_COLS
 PAIRS = CLASSES // 2
 TAP_ORDER = [KS * (KS - 1 - a) + (KS - 1 - b) for b in range(KS) for a in range(KS)]
+RAW_TAP = TAP_ORDER[0]
 N_MOVE = 256
 
 FLOPS = 2 * PIX * CLS_COLS * C
@@ -44,7 +45,7 @@ def tile_patternconv_k_kernel(tc, x, weight, bias, out):
 
     with ExitStack() as ctx:
         const = ctx.enter_context(tc.tile_pool(name="const", bufs=1))
-        loads = ctx.enter_context(tc.tile_pool(name="loads", bufs=4))
+        loads = ctx.enter_context(tc.tile_pool(name="loads", bufs=5))
         stage = ctx.enter_context(tc.tile_pool(name="stage", bufs=3))
         codes = ctx.enter_context(tc.tile_pool(name="codes", bufs=3))
         flip_psum = ctx.enter_context(tc.psum_pool(name="flip_psum", bufs=4))
@@ -94,6 +95,8 @@ def tile_patternconv_k_kernel(tc, x, weight, bias, out):
                         "k p (d e) o -> k p d (e o)", d=2
                     ),
                 )
+        raw_perm = const.tile([P, P], BF16)
+        nc.vector.tensor_copy(out=raw_perm[:], in_=perm[:, RAW_TAP, :])
         is_e = const.tile([P, 2], F32)
         ident_ije = ident[:].rearrange("k (n e) -> k e n", e=2)
         for e in range(2):
@@ -138,7 +141,15 @@ def tile_patternconv_k_kernel(tc, x, weight, bias, out):
             w_grp_words = w_grp[:].bitcast(F32).rearrange(
                 "k (c t o u) -> k t c o u", c=CLASSES, t=TAPS, o=O, u=2
             )
-            for n0 in range(0, TAPS, 2):
+            w_nat = held["w_nat", g][:].rearrange("p (k s t) -> p s t k", s=4, t=TAPS)
+            flipped = flip_psum.tile([P, 4, P], BF16, tag="flipped")
+            for s in range(4):
+                nc.tensor.transpose(flipped[:, s, :], w_nat[:, s, RAW_TAP, :], raw_perm[:])
+            nc.scalar.copy(
+                out=w_grp[:].rearrange("k (c t o s) -> k t c o s", c=CLASSES, t=TAPS, s=4)[:, 0],
+                in_=flipped[:].rearrange("k s (c o) -> k c o s", c=CLASSES),
+            )
+            for n0 in range(1, TAPS, 2):
                 flipped = flip_psum.tile([P, 2, 2, P], F32, tag="flipped")
                 taps_here = TAP_ORDER[n0 : n0 + 2]
                 for n, tap in enumerate(taps_here):
@@ -202,7 +213,7 @@ def tile_patternconv_k_kernel(tc, x, weight, bias, out):
                 held["x_grp", step] = stage.tile([P, PIX, 4], BF16, align_bytes=64, name="x_grp")
                 sort_taps(step, slice(0, 3), nc.vector.tensor_copy, pieces)
                 sort_taps(step, slice(3, 6), nc.scalar.copy, pieces)
-                sort_taps(step, slice(6, 9), nc.scalar.copy, pieces)
+                sort_taps(step, slice(6, RAW_TAP), nc.scalar.copy, pieces)
                 group_x(step, 0, pieces)
                 group_x(step, 1, pieces)
             if 0 <= step - 1 < PASSES:

@@ -128,8 +128,8 @@ def tile_patternconv_k_kernel(tc, x, weight, bias, out):
                 engine_copy(out=w_tap[:, :, ks, :, taps], in_=w_nat[:, :, ks, :, taps])
 
         def group_x(g, p, pieces):
-            x_raw = held["x_raw", g][:].rearrange("k t (i p j d e) -> k p i j t d e", i=BLK, p=PAT, j=BLK, d=2)
-            x_grp = held["x_grp", g][:].rearrange("k (d p i j e) t -> k p i j t d e", d=2, p=PAT, i=BLK, j=BLK)
+            x_raw = held["x_raw", g][:].rearrange("k t (i p j d e) -> k p i j d t e", i=BLK, p=PAT, j=BLK, d=2)
+            x_grp = held["x_grp", g][:].rearrange("k (d p i j e) t -> k p i j d t e", d=2, p=PAT, i=BLK, j=BLK)
             rows = BLK // pieces
             for n in range(pieces):
                 i_rows = slice(rows * n, rows * (n + 1))

@@ -28,6 +28,7 @@ W_COLS = CLASSES * CLS_COLS
 PAIRS = CLASSES // 2
 TAP_ORDER = [KS * (KS - 1 - a) + (KS - 1 - b) for b in range(KS) for a in range(KS)]
 RAW_TAP = TAP_ORDER[0]
+AHEAD = 3
 N_MOVE = 256
 
 FLOPS = 2 * PIX * CLS_COLS * C
@@ -54,22 +55,23 @@ def tile_patternconv_k_kernel(tc, x, weight, bias, out):
 
         held = {}
 
-        def load(g, pieces):
+        def load(g, x_pieces, w_pieces):
             w_nat = loads.tile([P, K_PASS * TAPS], BF16)
             x_raw = loads.tile([P, 4, PIX], BF16)
-            w_cols = K_PASS * TAPS // pieces
-            x_cols = PIX // pieces
-            for n in range(pieces):
-                cols = slice(w_cols * n, w_cols * (n + 1))
-                nc.sync.dma_start(out=w_nat[:, cols], in_=w_view[g][:, cols])
+            w_cols = K_PASS * TAPS // w_pieces
+            x_cols = PIX // x_pieces
+            for n in range(x_pieces):
+                for m in range(w_pieces // x_pieces * n, w_pieces // x_pieces * (n + 1)):
+                    cols = slice(w_cols * m, w_cols * (m + 1))
+                    nc.sync.dma_start(out=w_nat[:, cols], in_=w_view[g][:, cols])
                 cols = slice(x_cols * n, x_cols * (n + 1))
                 nc.sync.dma_start(out=x_raw[:, :, cols], in_=x_view[g][:, :, cols])
             held["w_nat", g] = w_nat
             held["x_raw", g] = x_raw
 
-        AHEAD = 3
-        for g in range(AHEAD):
-            load(g, 2 if g == 0 else 1)
+        load(0, 2, 4)
+        for g in range(1, AHEAD):
+            load(g, 1, 1)
 
         ident = const.tile([P, P], F32)
         make_identity(nc, ident[:])
@@ -119,21 +121,17 @@ def tile_patternconv_k_kernel(tc, x, weight, bias, out):
                 )
         z_banks = [z_psum.tile([P, 2, N_MOVE], F32, name="z_bank%d" % p) for p in range(PAT)]
 
-        def sort_taps(g, taps, engine_copy, pieces):
+        def sort_taps(g, taps, engine_copy, n=0, pieces=1):
             w_nat = held["w_nat", g][:].rearrange("p (k u e t) -> p u k e t", k=P, u=2, e=2)
             w_tap = held["w_tap", g][:].rearrange("p t (u k e) -> p u k e t", u=2, e=2)
-            rows = P // pieces
-            for n in range(pieces):
-                ks = slice(rows * n, rows * (n + 1))
-                engine_copy(out=w_tap[:, :, ks, :, taps], in_=w_nat[:, :, ks, :, taps])
+            ks = slice(P // pieces * n, P // pieces * (n + 1))
+            engine_copy(out=w_tap[:, :, ks, :, taps], in_=w_nat[:, :, ks, :, taps])
 
-        def group_x(g, p, pieces):
+        def group_x(g, p, n=0, pieces=1):
             x_raw = held["x_raw", g][:].rearrange("k t (i p j d e) -> k p i j d t e", i=BLK, p=PAT, j=BLK, d=2)
             x_grp = held["x_grp", g][:].rearrange("k (d p i j e) t -> k p i j d t e", d=2, p=PAT, i=BLK, j=BLK)
-            rows = BLK // pieces
-            for n in range(pieces):
-                i_rows = slice(rows * n, rows * (n + 1))
-                nc.vector.tensor_copy(out=x_grp[:, p, i_rows], in_=x_raw[:, p, i_rows])
+            i_rows = slice(BLK // pieces * n, BLK // pieces * (n + 1))
+            nc.vector.tensor_copy(out=x_grp[:, p, i_rows], in_=x_raw[:, p, i_rows])
 
         def flip(g):
             w_tap_words = held["w_tap", g][:].bitcast(F32)
@@ -146,8 +144,8 @@ def tile_patternconv_k_kernel(tc, x, weight, bias, out):
             for s in range(4):
                 nc.tensor.transpose(flipped[:, s, :], w_nat[:, s, RAW_TAP, :], raw_perm[:])
             nc.scalar.copy(
-                out=w_grp[:].rearrange("k (c t o s) -> k t c o s", c=CLASSES, t=TAPS, s=4)[:, 0],
-                in_=flipped[:].rearrange("k s (c o) -> k c o s", c=CLASSES),
+                out=w_grp[:].rearrange("k (c t o s) -> k t c s o", c=CLASSES, t=TAPS, s=4)[:, 0],
+                in_=flipped[:].rearrange("k s (c o) -> k c s o", c=CLASSES),
             )
             for n0 in range(1, TAPS, 2):
                 flipped = flip_psum.tile([P, 2, 2, P], F32, tag="flipped")
@@ -159,7 +157,8 @@ def tile_patternconv_k_kernel(tc, x, weight, bias, out):
                             w_tap_words[:, tap, P * u : P * (u + 1)],
                             perm[:, tap, :],
                         )
-                nc.scalar.copy(
+                copy = nc.vector.tensor_copy if g == PASSES - 1 and n0 > TAPS // 2 else nc.scalar.copy
+                copy(
                     out=w_grp_words[:, n0 : n0 + len(taps_here)],
                     in_=flipped[:, 0 : len(taps_here)].rearrange("k t u (c o) -> k t c o u", c=CLASSES),
                 )
@@ -204,28 +203,45 @@ def tile_patternconv_k_kernel(tc, x, weight, bias, out):
                         stop=(g == PASSES - 1 and d == 1),
                     )
 
-        for step in range(PASSES + 2):
-            pieces = 2 if step == 0 else 1
-            if AHEAD <= step + AHEAD - 1 < PASSES:
-                load(step + AHEAD - 1, 1)
+        def sort_all(g, n=0, pieces=1):
+            sort_taps(g, slice(0, 3), nc.vector.tensor_copy, n, pieces)
+            sort_taps(g, slice(3, 6), nc.scalar.copy, n, pieces)
+            sort_taps(g, slice(6, RAW_TAP), nc.scalar.copy, n, pieces)
+
+        def open_stage(g):
+            held["w_tap", g] = stage.tile([P, TAPS, K_PASS], BF16, align_bytes=64, name="w_tap")
+            held["x_grp", g] = stage.tile([P, PIX, 4], BF16, align_bytes=64, name="x_grp")
+
+        open_stage(0)
+        for n in range(2):
+            sort_all(0, 2 * n, 4)
+            sort_all(0, 2 * n + 1, 4)
+            for p in range(PAT):
+                group_x(0, p, n, 2)
+        load(AHEAD, 1, 1)
+        flip(0)
+        quantise_x(0)
+        for step in range(1, PASSES + 2):
+            if step + AHEAD < PASSES:
+                load(step + AHEAD, 1, 1)
             if step < PASSES:
-                held["w_tap", step] = stage.tile([P, TAPS, K_PASS], BF16, align_bytes=64, name="w_tap")
-                held["x_grp", step] = stage.tile([P, PIX, 4], BF16, align_bytes=64, name="x_grp")
-                sort_taps(step, slice(0, 3), nc.vector.tensor_copy, pieces)
-                sort_taps(step, slice(3, 6), nc.scalar.copy, pieces)
-                sort_taps(step, slice(6, RAW_TAP), nc.scalar.copy, pieces)
-                group_x(step, 0, pieces)
-                group_x(step, 1, pieces)
-            if 0 <= step - 1 < PASSES:
+                open_stage(step)
+                sort_all(step)
+                group_x(step, 0)
+                group_x(step, 1)
+            if 0 < step - 1 < PASSES - 1:
                 flip(step - 1)
             if 0 <= step - 2 < PASSES:
                 quantise_w(step - 2, (0, 512, 1024, W_COLS) if step - 2 == PASSES - 1 else (0, 1024, W_COLS))
-                multiply(step - 2)
             if step < PASSES:
-                group_x(step, 2, pieces)
-                group_x(step, 3, pieces)
-            if 0 <= step - 1 < PASSES:
+                group_x(step, 2)
+                group_x(step, 3)
+            if 0 < step - 1 < PASSES:
                 quantise_x(step - 1)
+            if step - 1 == PASSES - 1:
+                flip(step - 1)
+            if 0 <= step - 2 < PASSES:
+                multiply(step - 2)
 
         for p in range(PAT):
             for e in range(2):

@@ -57,15 +57,14 @@ def tile_patternconv_k_kernel(tc, x, weight, bias, out):
 
         def load(g, x_pieces, w_pieces):
             w_nat = loads.tile([P, K_PASS * TAPS], BF16)
-            x_raw = loads.tile([P, 4, PIX], BF16)
+            x_raw = loads.tile([P, x_pieces, 4, PIX // x_pieces], BF16, tag="x_raw")
             w_cols = K_PASS * TAPS // w_pieces
             x_cols = PIX // x_pieces
             for n in range(x_pieces):
                 for m in range(w_pieces // x_pieces * n, w_pieces // x_pieces * (n + 1)):
                     cols = slice(w_cols * m, w_cols * (m + 1))
                     nc.sync.dma_start(out=w_nat[:, cols], in_=w_view[g][:, cols])
-                cols = slice(x_cols * n, x_cols * (n + 1))
-                nc.sync.dma_start(out=x_raw[:, :, cols], in_=x_view[g][:, :, cols])
+                nc.sync.dma_start(out=x_raw[:, n], in_=x_view[g][:, :, x_cols * n : x_cols * (n + 1)])
             held["w_nat", g] = w_nat
             held["x_raw", g] = x_raw
 
@@ -75,8 +74,9 @@ def tile_patternconv_k_kernel(tc, x, weight, bias, out):
 
         ident = const.tile([P, P], F32)
         make_identity(nc, ident[:])
-        patch = const.tile([P, 2 * PAT, 2 * PAT * O], F32)
-        nc.gpsimd.memset(patch[:], 0.0)
+        padded = const.tile([P, 2 + 2 * PAT, 2 * PAT * O], F32)
+        nc.gpsimd.memset(padded[:], 0.0)
+        patch = padded[:, 2:]
         outer = const.tile([P, 2 * P - PAT * O], F32)
         nc.gpsimd.memset(outer[:], 0.0)
         bias_rows = const.tile([P, CLASSES * O], BF16)
@@ -128,10 +128,10 @@ def tile_patternconv_k_kernel(tc, x, weight, bias, out):
             engine_copy(out=w_tap[:, :, ks, :, taps], in_=w_nat[:, :, ks, :, taps])
 
         def group_x(g, p, n=0, pieces=1):
-            x_raw = held["x_raw", g][:].rearrange("k t (i p j d e) -> k p i j d t e", i=BLK, p=PAT, j=BLK, d=2)
-            x_grp = held["x_grp", g][:].rearrange("k (d p i j e) t -> k p i j d t e", d=2, p=PAT, i=BLK, j=BLK)
             i_rows = slice(BLK // pieces * n, BLK // pieces * (n + 1))
-            nc.vector.tensor_copy(out=x_grp[:, p, i_rows], in_=x_raw[:, p, i_rows])
+            x_raw = held["x_raw", g][:, n].rearrange("k t (i p j d e) -> k p i j t d e", p=PAT, j=BLK, d=2, e=2)
+            x_grp = held["x_grp", g][:].rearrange("k (d p i j e) t -> k p i j t d e", d=2, p=PAT, i=BLK, j=BLK)
+            nc.vector.tensor_copy(out=x_grp[:, p, i_rows], in_=x_raw[:, p])
 
         def flip(g):
             w_tap_words = held["w_tap", g][:].bitcast(F32)
@@ -157,8 +157,7 @@ def tile_patternconv_k_kernel(tc, x, weight, bias, out):
                             w_tap_words[:, tap, P * u : P * (u + 1)],
                             perm[:, tap, :],
                         )
-                copy = nc.vector.tensor_copy if g == PASSES - 1 and n0 > TAPS // 2 else nc.scalar.copy
-                copy(
+                nc.scalar.copy(
                     out=w_grp_words[:, n0 : n0 + len(taps_here)],
                     in_=flipped[:, 0 : len(taps_here)].rearrange("k t u (c o) -> k t c o u", c=CLASSES),
                 )
@@ -227,21 +226,23 @@ def tile_patternconv_k_kernel(tc, x, weight, bias, out):
             if step < PASSES:
                 open_stage(step)
                 sort_all(step)
+            if step == 1:
+                quantise_w(0, (0, 1024, W_COLS))
+            if step < PASSES:
                 group_x(step, 0)
                 group_x(step, 1)
-            if 0 < step - 1 < PASSES - 1:
+            if 0 < step - 1 < PASSES:
                 flip(step - 1)
-            if 0 <= step - 2 < PASSES:
+            if 0 < step - 2 < PASSES:
                 quantise_w(step - 2, (0, 512, 1024, W_COLS) if step - 2 == PASSES - 1 else (0, 1024, W_COLS))
             if step < PASSES:
                 group_x(step, 2)
                 group_x(step, 3)
             if 0 < step - 1 < PASSES:
                 quantise_x(step - 1)
-            if step - 1 == PASSES - 1:
-                flip(step - 1)
-            if 0 <= step - 2 < PASSES:
-                multiply(step - 2)
+            if 0 <= step - 3:
+                multiply(step - 3)
+        multiply(PASSES - 1)
 
         for p in range(PAT):
             for e in range(2):
@@ -262,14 +263,13 @@ def tile_patternconv_k_kernel(tc, x, weight, bias, out):
         )
 
         total = flip_psum.tile([P, PAT, PAT * O], F32, tag="flipped")
-        terms = [(di, dj) for dj in range(2) for di in range(2)]
+        terms = [(di, dj) for dj in (1, 0) for di in range(2)]
         for n, (di, dj) in enumerate(terms):
-            w0 = 2 * dj
-            rows = slice(PAT * O * (1 - di), PAT * O * (2 - di))
+            first_col = 0 if dj else 2 + PAT
             nc.tensor.matmul(
-                total[:, w0:PAT, :],
+                total[:],
                 lhsT=shift[:, 2 * di + dj, :],
-                rhs=patch[:, 0:2, rows] if dj else patch[:, PAT : 2 * PAT, rows],
+                rhs=padded[:, first_col : first_col + PAT, PAT * O * (1 - di) : PAT * O * (2 - di)],
                 start=(n == 0),
                 stop=(n == len(terms) - 1),
             )

from contextlib import ExitStack

import concourse.mybir as mybir
from concourse.masks import make_identity

F32 = mybir.dt.float32
BF16 = mybir.dt.bfloat16
U32 = mybir.dt.uint32
U8 = mybir.dt.uint8
FP8X4 = mybir.dt.float8_e4m3fn_x4
ADD = mybir.AluOpType.add
MULT = mybir.AluOpType.mult
AXIS_X = mybir.AxisListType.X

P = 128
C = 8192
K_PASS = 512
PASSES = C // K_PASS
PIX = 1024
PAT = 4
BLK = 8
CLASSES = PAT * PAT
O = 8
KS = 3
TAPS = KS * KS
CLS_COLS = TAPS * O
W_COLS = CLASSES * CLS_COLS
PAIRS = CLASSES // 2
TAP_ORDER = [KS * (KS - 1 - a) + (KS - 1 - b) for b in range(KS) for a in range(KS)]
RAW_TAP = TAP_ORDER[0]
AHEAD = 3
N_MOVE = 256

FLOPS = 2 * PIX * CLS_COLS * C


def window_of(pair):
    return min(2 * CLS_COLS * pair // 64 * 64, W_COLS - N_MOVE)


def tile_patternconv_k_kernel(tc, x, weight, bias, out):
    nc = tc.nc
    x_view = x.rearrange("b (g k t) y z -> g k t (b y z)", g=PASSES, k=P, t=4)
    w_view = weight.rearrange("h w o (g c) u v -> g (h w o) (c u v)", g=PASSES)
    out_view = out.rearrange("b o (i h) z -> h (b o) i z", h=PAT)

    with ExitStack() as ctx:
        const = ctx.enter_context(tc.tile_pool(name="const", bufs=1))
        loads = ctx.enter_context(tc.tile_pool(name="loads", bufs=5))
        stage = ctx.enter_context(tc.tile_pool(name="stage", bufs=3))
        codes = ctx.enter_context(tc.tile_pool(name="codes", bufs=3))
        flip_psum = ctx.enter_context(tc.psum_pool(name="flip_psum", bufs=4))
        z_psum = ctx.enter_context(tc.psum_pool(name="z_psum", bufs=1))
        ctx.enter_context(tc.manual_schedule())

        held = {}

        def load(g, x_pieces, w_pieces):
            w_nat = loads.tile([P, K_PASS * TAPS], BF16)
            x_raw = loads.tile([P, x_pieces, 4, PIX // x_pieces], BF16, tag="x_raw")
            w_cols = K_PASS * TAPS // w_pieces
            x_cols = PIX // x_pieces
            for n in range(x_pieces):
                for m in range(w_pieces // x_pieces * n, w_pieces // x_pieces * (n + 1)):
                    cols = slice(w_cols * m, w_cols * (m + 1))
                    nc.sync.dma_start(out=w_nat[:, cols], in_=w_view[g][:, cols])
                nc.sync.dma_start(out=x_raw[:, n], in_=x_view[g][:, :, x_cols * n : x_cols * (n + 1)])
            held["w_nat", g] = w_nat
            held["x_raw", g] = x_raw

        load(0, 2, 4)
        for g in range(1, AHEAD):
            load(g, 1, 1)

        ident = const.tile([P, P], F32)
        make_identity(nc, ident[:])
        padded = const.tile([P, 2 + 2 * PAT, 2 * PAT * O], F32)
        nc.gpsimd.memset(padded[:], 0.0)
        patch = padded[:, 2:]
        outer = const.tile([P, 2 * P - PAT * O], F32)
        nc.gpsimd.memset(outer[:], 0.0)
        bias_rows = const.tile([P, CLASSES * O], BF16)
        nc.scalar.dma_start(out=bias_rows[:], in_=bias.rearrange("h w o -> (h w o)").partition_broadcast(P))
        twice = const.tile([P, 2 * PAT, 2 * PAT, O], F32)
        ident_hwo = ident[:].rearrange("k (h w o) -> k h w o", h=PAT, w=PAT)
        for a in range(2):
            for b in range(2):
                nc.vector.tensor_copy(
                    out=twice[:, PAT * a : PAT * (a + 1), PAT * b : PAT * (b + 1), :], in_=ident_hwo
                )
        perm = const.tile([P, TAPS, P], F32)
        for u in range(KS):
            for v in range(KS):
                nc.vector.tensor_copy(
                    out=perm[:, KS * u + v, :].rearrange("k (d p e o) -> k p d (e o)", d=2, p=PAT, e=2),
                    in_=twice[:, PAT - u : 2 * PAT - u, PAT - v : 2 * PAT - v, :].rearrange(
                        "k p (d e) o -> k p d (e o)", d=2
                    ),
                )
        raw_perm = const.tile([P, P], BF16)
        nc.vector.tensor_copy(out=raw_perm[:], in_=perm[:, RAW_TAP, :])
        is_e = const.tile([P, 2], F32)
        ident_ije = ident[:].rearrange("k (n e) -> k e n", e=2)
        for e in range(2):
            nc.vector.tensor_reduce(out=is_e[:, e : e + 1], in_=ident_ije[:, e, :], op=ADD, axis=AXIS_X)
        block_of = const.tile([P, BLK + 1, BLK + 1], F32)
        nc.vector.memset(block_of[:], 0.0)
        nc.vector.tensor_tensor(
            out=block_of[:, 0:BLK, 0:BLK],
            in0=ident_ije[:, 0, :].rearrange("k (i j) -> k i j", i=BLK),
            in1=ident_ije[:, 1, :].rearrange("k (i j) -> k i j", i=BLK),
            op=ADD,
        )
        shift = const.tile([P, 4, P], F32)
        nc.vector.memset(shift[:], 0.0)
        for di in range(2):
            for dj in range(2):
                nc.vector.tensor_copy(
                    out=shift[:, 2 * di + dj, 0 : BLK * BLK].rearrange("k (i j) -> k i j", i=BLK),
                    in_=block_of[:, di : di + BLK, dj : dj + BLK],
                )
        z_banks = [z_psum.tile([P, 2, N_MOVE], F32, name="z_bank%d" % p) for p in range(PAT)]

        def sort_taps(g, taps, engine_copy, n=0, pieces=1):
            w_nat = held["w_nat", g][:].rearrange("p (k u e t) -> p u k e t", k=P, u=2, e=2)
            w_tap = held["w_tap", g][:].rearrange("p t (u k e) -> p u k e t", u=2, e=2)
            ks = slice(P // pieces * n, P // pieces * (n + 1))
            engine_copy(out=w_tap[:, :, ks, :, taps], in_=w_nat[:, :, ks, :, taps])

        def group_x(g, p, n=0, pieces=1):
            i_rows = slice(BLK // pieces * n, BLK // pieces * (n + 1))
            x_raw = held["x_raw", g][:, n].rearrange("k t (i p j d e) -> k p i j t d e", p=PAT, j=BLK, d=2, e=2)
            x_grp = held["x_grp", g][:].rearrange("k (d p i j e) t -> k p i j t d e", d=2, p=PAT, i=BLK, j=BLK)
            nc.vector.tensor_copy(out=x_grp[:, p, i_rows], in_=x_raw[:, p])

        def flip(g):
            w_tap_words = held["w_tap", g][:].bitcast(F32)
            w_grp = stage.tile([P, W_COLS * 4], BF16, align_bytes=64)
            w_grp_words = w_grp[:].bitcast(F32).rearrange(
                "k (c t o u) -> k t c o u", c=CLASSES, t=TAPS, o=O, u=2
            )
            w_nat = held["w_nat", g][:].rearrange("p (k s t) -> p s t k", s=4, t=TAPS)
            flipped = flip_psum.tile([P, 4, P], BF16, tag="flipped")
            for s in range(4):
                nc.tensor.transpose(flipped[:, s, :], w_nat[:, s, RAW_TAP, :], raw_perm[:])
            nc.scalar.copy(
                out=w_grp[:].rearrange("k (c t o s) -> k t c s o", c=CLASSES, t=TAPS, s=4)[:, 0],
                in_=flipped[:].rearrange("k s (c o) -> k c s o", c=CLASSES),
            )
            for n0 in range(1, TAPS, 2):
                flipped = flip_psum.tile([P, 2, 2, P], F32, tag="flipped")
                taps_here = TAP_ORDER[n0 : n0 + 2]
                for n, tap in enumerate(taps_here):
                    for u in range(2):
                        nc.tensor.transpose(
                            flipped[:, n, u, :],
                            w_tap_words[:, tap, P * u : P * (u + 1)],
                            perm[:, tap, :],
                        )
                nc.scalar.copy(
                    out=w_grp_words[:, n0 : n0 + len(taps_here)],
                    in_=flipped[:, 0 : len(taps_here)].rearrange("k t u (c o) -> k t c o u", c=CLASSES),
                )
            held["w_grp", g] = w_grp

        def quantise_x(g):
            x_codes = codes.tile([P, PIX], U32, align_bytes=64)
            x_scales = codes.tile([P, PIX], U8, align_bytes=64)
            nc.vector.quantize_mx(
                out=x_codes[:].bitcast(FP8X4),
                scales=x_scales[:],
                in_=held["x_grp", g][:].rearrange("k c t -> k (c t)"),
            )
            held["x_mx", g] = (x_codes, x_scales)

        def quantise_w(g, cuts):
            w_grp = held["w_grp", g]
            w_codes = codes.tile([P, W_COLS], U32, align_bytes=64)
            w_scales = codes.tile([P, W_COLS], U8, align_bytes=64)
            for c0, c1 in zip(cuts[:-1], cuts[1:]):
                nc.vector.quantize_mx(
                    out=w_codes[:, c0:c1].bitcast(FP8X4),
                    scales=w_scales[:, c0:c1],
                    in_=w_grp[:, 4 * c0 : 4 * c1],
                )
            held["w_mx", g] = (w_codes, w_scales)

        def multiply(g):
            x_codes, x_scales = held["x_mx", g]
            w_codes, w_scales = held["w_mx", g]
            for p in range(PAT):
                for d in range(2):
                    pair = PAT * d + p
                    window = window_of(pair)
                    nc.tensor.matmul_mx(
                        out=z_banks[p][:, d, :],
                        lhsT=x_codes[:, P * pair : P * (pair + 1)].bitcast(FP8X4),
                        lhsT_scale=x_scales[:, P * pair : P * (pair + 1)],
                        rhs=w_codes[:, window : window + N_MOVE].bitcast(FP8X4),
                        rhs_scale=w_scales[:, window : window + N_MOVE],
                        start=(g == 0 and d == 0),
                        stop=(g == PASSES - 1 and d == 1),
                    )

        def sort_all(g, n=0, pieces=1):
            sort_taps(g, slice(0, 3), nc.vector.tensor_copy, n, pieces)
            sort_taps(g, slice(3, 6), nc.scalar.copy, n, pieces)
            sort_taps(g, slice(6, RAW_TAP), nc.scalar.copy, n, pieces)

        def open_stage(g):
            held["w_tap", g] = stage.tile([P, TAPS, K_PASS], BF16, align_bytes=64, name="w_tap")
            held["x_grp", g] = stage.tile([P, PIX, 4], BF16, align_bytes=64, name="x_grp")

        open_stage(0)
        for n in range(2):
            sort_all(0, 2 * n, 4)
            sort_all(0, 2 * n + 1, 4)
            for p in range(PAT):
                group_x(0, p, n, 2)
        load(AHEAD, 1, 1)
        flip(0)
        quantise_x(0)
        for step in range(1, PASSES + 2):
            if step + AHEAD < PASSES:
                load(step + AHEAD, 1, 1)
            if step < PASSES:
                open_stage(step)
                sort_all(step)
            if step == 1:
                quantise_w(0, (0, 1024, W_COLS))
            if step < PASSES:
                group_x(step, 0)
                group_x(step, 1)
            if 0 < step - 1 < PASSES:
                flip(step - 1)
            if 0 < step - 2 < PASSES:
                quantise_w(step - 2, (0, 512, 1024, W_COLS) if step - 2 == PASSES - 1 else (0, 1024, W_COLS))
            if step < PASSES:
                group_x(step, 2)
                group_x(step, 3)
            if 0 < step - 1 < PASSES:
                quantise_x(step - 1)
            if 0 <= step - 3:
                multiply(step - 3)
        multiply(PASSES - 1)

        for p in range(PAT):
            for e in range(2):
                for d in range(2):
                    pair = PAT * d + p
                    mine = CLS_COLS * (2 * pair + e) - window_of(pair)
                    cell = patch[:, PAT * d + e : PAT * d + e + KS, O * (p + 2) : O * (p + 2 + KS)]
                    nc.vector.scalar_tensor_tensor(
                        out=cell,
                        in0=z_banks[p][:, d, mine : mine + CLS_COLS].rearrange("k (b n) -> k b n", b=KS),
                        scalar=is_e[:, e : e + 1],
                        in1=cell,
                        op0=MULT,
                        op1=ADD,
                    )
        nc.vector.tensor_tensor(
            out=patch[:, PAT : PAT + 2, :], in0=patch[:, PAT : PAT + 2, :], in1=patch[:, 2:PAT, :], op=ADD
        )

        total = flip_psum.tile([P, PAT, PAT * O], F32, tag="flipped")
        terms = [(di, dj) for dj in (1, 0) for di in range(2)]
        for n, (di, dj) in enumerate(terms):
            first_col = 0 if dj else 2 + PAT
            nc.tensor.matmul(
                total[:],
                lhsT=shift[:, 2 * di + dj, :],
                rhs=padded[:, first_col : first_col + PAT, PAT * O * (1 - di) : PAT * O * (2 - di)],
                start=(n == 0),
                stop=(n == len(terms) - 1),
            )
        nc.vector.tensor_tensor(
            out=outer[:, 0:P].rearrange("k (w h o) -> k w h o", w=PAT, h=PAT),
            in0=total[:].rearrange("k w (h o) -> k w h o", h=PAT),
            in1=bias_rows[:].rearrange("k (h w o) -> k w h o", h=PAT, w=PAT),
            op=ADD,
        )
        turned = flip_psum.tile([P, PAT, P], F32, tag="flipped")
        for w in range(PAT):
            nc.tensor.transpose(turned[:, w, :], outer[:, PAT * O * w : PAT * O * w + P], ident[:])
        result = const.tile([PAT * O, BLK * BLK, PAT], F32)
        nc.vector.tensor_copy(
            out=result[:], in_=turned[0 : PAT * O, :, 0 : BLK * BLK].rearrange("k w n -> k n w")
        )
        for h in range(PAT):
            queue = nc.sync if h % 2 == 0 else nc.scalar
            queue.dma_start(
                out=out_view[h],
                in_=result[O * h : O * (h + 1)].rearrange("k (i j) w -> k i (j w)", i=BLK),
            )
